import numpy as np
import ml_dtypes


def mxq(x, axis, fmt="e4m3"):
    dtype, down = {"e4m3": (ml_dtypes.float8_e4m3fn, 7), "e5m2": (ml_dtypes.float8_e5m2, 14)}[fmt]
    v = np.moveaxis(np.asarray(x, np.float32).astype(ml_dtypes.bfloat16).astype(np.float64), axis, -1)
    blocks = v.reshape(v.shape[:-1] + (-1, 32))
    amax = np.abs(blocks).max(-1, keepdims=True)
    byte = np.maximum(np.where(amax > 0, np.frexp(amax)[1] - 1 + 127, 0) - down, 1)
    scale = np.exp2(byte - 127.0)
    codes = (blocks / scale).astype(np.float32).astype(dtype).astype(np.float64)
    return np.moveaxis((codes * scale).reshape(v.shape), -1, axis)


WIDE = False


def mx_kscale(k):
    if not WIDE:
        return np.ones(k)
    levels = np.array([30, -30])
    if k % 512:
        return np.exp2(np.random.permutation(np.resize(levels, k // 32))).repeat(32)
    a = np.empty((k // 512, 16))
    for p in range(k // 512):
        a[p, :8] = np.random.permutation(np.resize(levels, 8))
        for g in range(8):
            far = levels[np.abs(levels - a[p, g]) >= 10]
            a[p, g + 8] = far[np.random.randint(len(far))]
    return np.exp2(a.ravel()).repeat(32)


BF16 = ml_dtypes.bfloat16


def bf(x):
    return np.asarray(x, np.float32).astype(BF16)


def f64(x):
    return np.asarray(x).astype(np.float64)


B, N, DIM, H, D, M = 2, 512, 1024, 16, 64, 16
HD = H * D
HALF = D // 2
EPS = 1e-12


def l2norm(t):
    n = np.sqrt((t * t).sum(-1, keepdims=True))
    return t / np.maximum(n, EPS)


def rope(t, fr):
    rot = np.concatenate([-t[..., HALF:], t[..., :HALF]], axis=-1)
    return t * np.cos(fr) + rot * np.sin(fr)


def heads(t):
    return t.reshape(B, N, H, D).transpose(0, 2, 1, 3)


def setup_inputs():
    s = mx_kscale(DIM)
    ang = np.random.uniform(-np.pi, np.pi, (N, HALF))
    return {"x": bf(np.random.standard_normal((B, N, DIM)) * s),
            "freqs": bf(np.concatenate([ang, ang], axis=-1)),
            "Wq": bf(np.random.standard_normal((DIM, HD)) / np.sqrt(DIM) / s[:, None]),
            "Wk": bf(np.random.standard_normal((DIM, HD)) / np.sqrt(DIM) / s[:, None]),
            "Wv": bf(np.random.standard_normal((DIM, HD)) / np.sqrt(DIM) / s[:, None]),
            "mem_k": bf(np.random.standard_normal((H, M, D))),
            "mem_v": bf(np.random.standard_normal((H, M, D)))}


def reference(x, freqs, Wq, Wk, Wv, mem_k, mem_v):
    xq = mxq(f64(x), 2, "e5m2")
    fr = f64(freqs)
    q = heads(xq @ mxq(f64(Wq), 0, "e5m2"))
    k = heads(xq @ mxq(f64(Wk), 0, "e5m2"))
    v = heads(xq @ mxq(f64(Wv), 0, "e5m2"))
    q = rope(l2norm(q), fr)
    k = rope(l2norm(k), fr)
    v = rope(v, fr)
    mk = np.broadcast_to(l2norm(f64(mem_k))[None], (B, H, M, D))
    mv = np.broadcast_to(f64(mem_v)[None], (B, H, M, D))
    return q, np.concatenate([mk, k], axis=2), np.concatenate([mv, v], axis=2)

@@ -1,0 +1,325 @@
+import math
+from contextlib import ExitStack
+
+import concourse.mybir as mybir
+from concourse.masks import make_identity
+
+B, N, DIM, H, D, MEM = 2, 512, 1024, 16, 64, 16
+FLOPS = 2 * B * N * DIM * 3 * H * D
+
+F32 = mybir.dt.float32
+BF16 = mybir.dt.bfloat16
+U32 = mybir.dt.uint32
+U8 = mybir.dt.uint8
+E5M2X4 = mybir.dt.float8_e5m2_x4
+ACT = mybir.ActivationFunctionType
+ALU = mybir.AluOpType
+
+P = 128
+PACK = 4
+K_PASS = P * PACK
+PASSES = DIM // K_PASS
+HALF = D // 2
+SLOTS = N // P
+TILES = B * SLOTS
+COLS = 512
+HEADS = COLS // D
+CHUNKS = 6
+STEPS = CHUNKS * TILES
+PLAIN_STEPS = 2 * TILES
+PIECE = 128
+PIECES = COLS // PIECE
+EPS_SQ = 1e-24
+MEM_Q = 4
+MEM_ROWS = MEM // MEM_Q
+BANKS = 8
+GROUPED_BUFS = 5
+PROD_BUFS = 3
+STAGE_BUFS = 4
+
+
+def tile_attention_pa_kernel(tc, x, freqs, Wq, Wk, Wv, mem_k, mem_v, out_0, out_1, out_2):
+    nc = tc.nc
+    weights = [Wv, Wq, Wk]
+    outs = [out_2, out_0, out_1]
+    first_row = [MEM, 0, MEM]
+
+    with ExitStack() as ctx:
+        keep = ctx.enter_context(tc.tile_pool(name="keep", bufs=1))
+        psum = ctx.enter_context(tc.psum_pool(name="psum", bufs=1))
+        ctx.enter_context(tc.manual_schedule())
+
+        angles = keep.tile([P, SLOTS, D], BF16)
+        abs_angles = keep.tile([P, SLOTS, D], F32)
+        trig = keep.tile([P, SLOTS, 2, D], F32)
+        ident = keep.tile([P, P], F32)
+        x_raw = keep.tile([P, TILES, DIM], BF16)
+        x_grouped = keep.tile([P, TILES, DIM], BF16, align_bytes=64)
+        x_codes = keep.tile([P, TILES, PASSES * P], U32, align_bytes=64)
+        x_scales = keep.tile([P, TILES, PASSES * P], U8, align_bytes=64)
+        wv_raw = keep.tile([P, 2, PASSES, PACK, COLS], BF16)
+        wqk_raw = keep.tile([P, 2, PASSES, PACK, DIM], BF16)
+        w_codes = keep.tile([P, CHUNKS, PASSES, COLS], U32, align_bytes=64)
+        w_scales = keep.tile([P, CHUNKS, PASSES, COLS], U8, align_bytes=64)
+        squares = keep.tile([P, 2, COLS], F32)
+        sumsq = keep.tile([P, STEPS - PLAIN_STEPS, HEADS], F32)
+        excess = keep.tile([P, STEPS - PLAIN_STEPS, HEADS], F32)
+        inv_norm = keep.tile([P, STEPS - PLAIN_STEPS, HEADS], F32)
+        memk_raw = keep.tile([H * MEM_Q, MEM_ROWS, D], BF16)
+        memv_raw = keep.tile([H * MEM_Q, MEM_ROWS, D], BF16)
+        memk_sq = keep.tile([H * MEM_Q, MEM_ROWS, D], F32)
+        memk_out = keep.tile([H * MEM_Q, MEM_ROWS, D], F32)
+        memv_out = keep.tile([H * MEM_Q, MEM_ROWS, D], F32)
+        memk_sumsq = keep.tile([H * MEM_Q, MEM_ROWS], F32)
+        memk_excess = keep.tile([H * MEM_Q, MEM_ROWS], F32)
+        memk_inv = keep.tile([H * MEM_Q, MEM_ROWS], F32)
+
+        banks_taken = []
+        grouped = {}
+        sums = {}
+        products = {}
+        staged = {}
+        stages_taken = []
+
+        def take_bank():
+            label = "bank%d" % (len(banks_taken) % BANKS)
+            bank = psum.tile([P, COLS], F32, name=label, tag=label)
+            banks_taken.append(bank)
+            return bank
+
+        def load_x(i):
+            b, j = divmod(i, SLOTS)
+            rows = x[b].rearrange("(p j) k -> p j k", j=SLOTS)
+            nc.sync.dma_start(out=x_raw[:, i, :], in_=rows[:, j, :])
+
+        def w_rows(m, g):
+            return weights[m][g * K_PASS : (g + 1) * K_PASS, :].rearrange("(p t) n -> p t n", t=PACK)
+
+        def load_wv(half, g):
+            nc.sync.dma_start(out=wv_raw[:, half, g], in_=w_rows(0, g)[:, :, half * COLS : (half + 1) * COLS])
+
+        def load_wqk(m, g):
+            nc.sync.dma_start(out=wqk_raw[:, m - 1, g], in_=w_rows(m, g))
+
+        def turn_x(i):
+            bank = take_bank()
+            words = x_raw[:, i, :].bitcast(F32)
+            for g in range(PASSES):
+                for u in range(2):
+                    at = (2 * g + u) * P
+                    nc.tensor.transpose(
+                        bank[:, at : at + P], words[:, 2 * P * g + u : 2 * P * (g + 1) : 2], ident[:]
+                    )
+            nc.scalar.copy(
+                out=x_grouped[:, i, :].bitcast(F32).rearrange("p (g r u) -> p g r u", g=PASSES, u=2),
+                in_=bank[:].rearrange("p (g u r) -> p g r u", g=PASSES, u=2),
+            )
+
+        def quantize_x(i, count):
+            nc.vector.quantize_mx(
+                out=x_codes[:, i : i + count, :].rearrange("p i w -> p (i w)").bitcast(E5M2X4),
+                scales=x_scales[:, i : i + count, :].rearrange("p i w -> p (i w)"),
+                in_=x_grouped[:, i : i + count, :].rearrange("p i k -> p (i k)"),
+            )
+
+        def interleave_w(copy, c, g, start, width):
+            if (c, g) not in grouped:
+                label = "grouped%d" % (len(grouped) % GROUPED_BUFS)
+                grouped[(c, g)] = keep.tile([P, COLS, PACK], BF16, name=label, tag=label, align_bytes=64)
+            m, half = divmod(c, 2)
+            if m == 0:
+                src = wv_raw[:, half, g, :, start : start + width]
+            else:
+                src = wqk_raw[:, m - 1, g, :, half * COLS + start : half * COLS + start + width]
+            copy(
+                out=grouped[(c, g)][:, start : start + width, :].rearrange("p (c i) t -> p c t i", i=4),
+                in_=src.rearrange("p t (c i) -> p c t i", i=4),
+            )
+
+        def quantize_w(c, g):
+            nc.vector.quantize_mx(
+                out=w_codes[:, c, g, :].bitcast(E5M2X4),
+                scales=w_scales[:, c, g, :],
+                in_=grouped[(c, g)][:].rearrange("p n t -> p (n t)"),
+            )
+
+        def project(s):
+            c, i = divmod(s, TILES)
+            sums[s] = take_bank()
+            for g in range(PASSES):
+                nc.tensor.matmul_mx(
+                    out=sums[s][:],
+                    lhsT=x_codes[:, i, g * P : (g + 1) * P].bitcast(E5M2X4),
+                    lhsT_scale=x_scales[:, i, g * P : (g + 1) * P],
+                    rhs=w_codes[:, c, g, :].bitcast(E5M2X4),
+                    rhs_scale=w_scales[:, c, g, :],
+                    start=(g == 0),
+                    stop=(g == PASSES - 1),
+                )
+
+        def sum_squares(s, heads):
+            for h in heads:
+                nc.scalar.activation(
+                    out=squares[:, s % 2, h * D : (h + 1) * D],
+                    in_=sums[s][:, h * D : (h + 1) * D],
+                    func=ACT.Square,
+                    accum_out=sumsq[:, s - PLAIN_STEPS, h : h + 1],
+                )
+
+        def above_floor(dst, src):
+            nc.scalar.activation(out=dst, in_=src, func=ACT.Relu, bias=-EPS_SQ)
+
+        def inverse_root(dst, src):
+            nc.scalar.activation(out=dst, in_=src, func=ACT.Abs_reciprocal_sqrt, bias=EPS_SQ)
+
+        def multiply(s):
+            j = s % SLOTS
+            if s % 2 == 0:
+                label = "products%d" % (len(products) % PROD_BUFS)
+                products[s // 2] = keep.tile([P, 2, HEADS, 2, D], F32, name=label, tag=label)
+            dst = products[s // 2][:, s % 2]
+            if s < PLAIN_STEPS:
+                nc.vector.tensor_tensor(
+                    out=dst,
+                    in0=sums[s][:].rearrange("p (h d) -> p h d", d=D).unsqueeze(2).to_broadcast([P, HEADS, 2, D]),
+                    in1=trig[:, j].unsqueeze(1).to_broadcast([P, HEADS, 2, D]),
+                    op=ALU.mult,
+                )
+            else:
+                for h in range(HEADS):
+                    nc.vector.scalar_tensor_tensor(
+                        out=dst[:, h],
+                        in0=sums[s][:, h * D : (h + 1) * D].unsqueeze(1).to_broadcast([P, 2, D]),
+                        scalar=inv_norm[:, s - PLAIN_STEPS, h : h + 1],
+                        in1=trig[:, j],
+                        op0=ALU.mult,
+                        op1=ALU.mult,
+                    )
+
+        def add_pair(engine, s):
+            group, j = divmod(s - 1, SLOTS)
+            if j == 0 or s == STEPS - 1:
+                label = "staged%d" % (len(stages_taken) % STAGE_BUFS)
+                staged[group] = keep.tile([P, HEADS, SLOTS, D], F32, name=label, tag=label)
+                stages_taken.append(staged[group])
+            pair = products[s // 2]
+            for half in range(2):
+                here = slice(half * HALF, (half + 1) * HALF)
+                other = slice((1 - half) * HALF, (2 - half) * HALF)
+                engine.tensor_tensor(
+                    out=staged[group][:, :, j : j + 2, here].rearrange("p h j d -> p j h d"),
+                    in0=pair[:, :, :, 0, here],
+                    in1=pair[:, :, :, 1, other],
+                    op=ALU.add,
+                )
+
+        def store(group, slots):
+            c, b = divmod(group, B)
+            m, half = divmod(c, 2)
+            rows = outs[m][b, half * HEADS : (half + 1) * HEADS, first_row[m] : first_row[m] + N, :]
+            rows = rows.rearrange("h (p j) d -> p h j d", j=SLOTS)
+            nc.sync.dma_start(
+                out=rows[:, :, slots, :].rearrange("p h j d -> p h (j d)"),
+                in_=staged[group][:, :, slots, :].rearrange("p h j d -> p h (j d)"),
+            )
+
+        def memory_rows():
+            for r in range(MEM_ROWS):
+                nc.scalar.activation(
+                    out=memk_sq[:, r, :], in_=memk_raw[:, r, :], func=ACT.Square, accum_out=memk_sumsq[:, r : r + 1]
+                )
+            nc.scalar.copy(out=memv_out[:], in_=memv_raw[:])
+            above_floor(memk_excess[:], memk_sumsq[:])
+            inverse_root(memk_inv[:], memk_excess[:])
+            for r in range(MEM_ROWS):
+                nc.scalar.activation(
+                    out=memk_out[:, r, :], in_=memk_raw[:, r, :], func=ACT.Copy, scale=memk_inv[:, r : r + 1]
+                )
+            for dst, src in ((out_2, memv_out), (out_1, memk_out)):
+                for q in range(MEM_Q):
+                    rows = dst[:, :, q * MEM_ROWS : (q + 1) * MEM_ROWS, :].rearrange("b h m d -> h b (m d)")
+                    part = src[q : H * MEM_Q : MEM_Q].rearrange("h m d -> h (m d)")
+                    nc.sync.dma_start(out=rows, in_=part.unsqueeze(1).to_broadcast([H, B, MEM_ROWS * D]))
+
+        nc.sync.dma_start(out=angles[:], in_=freqs.rearrange("(p j) d -> p j d", j=SLOTS))
+        load_wv(0, 0)
+        load_wv(0, 1)
+        for i in range(3):
+            load_x(i)
+        nc.sync.dma_start(out=memk_raw[:], in_=mem_k.rearrange("h (q m) d -> (h q) m d", q=MEM_Q))
+        nc.sync.dma_start(out=memv_raw[:], in_=mem_v.rearrange("h (q m) d -> (h q) m d", q=MEM_Q))
+        load_wv(1, 0)
+        for i in range(3, 6):
+            load_x(i)
+        load_wv(1, 1)
+        for i in range(6, TILES):
+            load_x(i)
+        for m in (1, 2):
+            for g in range(PASSES):
+                load_wqk(m, g)
+
+        make_identity(nc, ident[:])
+
+        nc.scalar.activation(out=trig[:, :, 1, 0:HALF], in_=angles[:, :, HALF:D], func=ACT.Sin)
+        nc.scalar.activation(out=trig[:, :, 1, HALF:D], in_=angles[:, :, 0:HALF], func=ACT.Sin, scale=-1.0)
+        nc.scalar.activation(out=abs_angles[:], in_=angles[:], func=ACT.Abs)
+        nc.scalar.activation(out=trig[:, :, 0, :], in_=abs_angles[:], func=ACT.Sin, scale=-1.0, bias=math.pi / 2)
+
+        for g in range(PASSES):
+            interleave_w(nc.vector.tensor_copy, 0, g, 0, COLS)
+        for i in range(3):
+            turn_x(i)
+        for g in range(PASSES):
+            quantize_w(0, g)
+        quantize_x(0, 1)
+        quantize_x(1, 1)
+        project(0)
+        turn_x(3)
+        project(1)
+
+        pieces = [(c, g, k) for c in range(1, CHUNKS) for g in range(PASSES) for k in range(PIECES)]
+        per_chunk = PASSES * PIECES
+        piece_step = (
+            [max(n - 2, -1) for n in range(per_chunk)]
+            + [6 + n // 2 for n in range(2 * per_chunk)]
+            + [14 + 3 * n // 2 for n in range(2 * per_chunk)]
+        )
+
+        def interleave_pieces(s):
+            for n, (c, g, k) in enumerate(pieces):
+                if piece_step[n] == s:
+                    interleave_w(nc.scalar.copy, c, g, k * PIECE, PIECE)
+
+        interleave_pieces(-1)
+        turn_at = {0: (4, 5), 1: (6,), 2: (7,)}
+        quantize_at = {0: 2, 1: 4, 3: 6}
+        for s in range(STEPS):
+            c, i = divmod(s, TILES)
+            for t in turn_at.get(s, ()):
+                turn_x(t)
+            if s == 3:
+                memory_rows()
+            interleave_pieces(s)
+            multiply(s)
+            if s in quantize_at:
+                quantize_x(quantize_at[s], 2)
+            if c + 1 < CHUNKS and i in (3, 5):
+                quantize_w(c + 1, (i - 3) // 2)
+            if s % 2 == 1:
+                add_pair(nc.vector if s == STEPS - 1 else nc.gpsimd, s)
+            if s == STEPS - 3:
+                store(s // SLOTS, slice(0, 2))
+            elif s == STEPS - 1:
+                store(s // SLOTS, slice(2, SLOTS))
+            elif s % SLOTS == SLOTS - 1:
+                store(s // SLOTS, slice(0, SLOTS))
+            if s + 2 < STEPS:
+                project(s + 2)
+            if PLAIN_STEPS <= s + 2 < STEPS:
+                sum_squares(s + 2, range(0, HEADS // 2))
+            if PLAIN_STEPS <= s + 1 < STEPS:
+                above_floor(excess[:, s + 1 - PLAIN_STEPS, :], sumsq[:, s + 1 - PLAIN_STEPS, :])
+            if PLAIN_STEPS <= s + 2 < STEPS:
+                sum_squares(s + 2, range(HEADS // 2, HEADS))
+            if PLAIN_STEPS <= s + 1 < STEPS:
+                inverse_root(inv_norm[:, s + 1 - PLAIN_STEPS, :], excess[:, s + 1 - PLAIN_STEPS, :])

@@ -33,7 +33,7 @@ EPS_SQ = 1e-24
 MEM_Q = 4
 MEM_ROWS = MEM // MEM_Q
 BANKS = 8
-GROUPED_BUFS = 5
+GROUPED_BUFS = 4
 PROD_BUFS = 3
 STAGE_BUFS = 4
 
@@ -78,8 +78,7 @@ def tile_attention_pa_kernel(tc, x, freqs, Wq, Wk, Wv, mem_k, mem_v, out_0, out_
         grouped = {}
         sums = {}
         products = {}
-        staged = {}
-        stages_taken = []
+        staged = []
 
         def take_bank():
             label = "bank%d" % (len(banks_taken) % BANKS)
@@ -174,53 +173,48 @@ def tile_attention_pa_kernel(tc, x, freqs, Wq, Wk, Wv, mem_k, mem_v, out_0, out_
 
         def multiply(s):
             j = s % SLOTS
-            if s % 2 == 0:
+            if j == 0:
                 label = "products%d" % (len(products) % PROD_BUFS)
-                products[s // 2] = keep.tile([P, 2, HEADS, 2, D], F32, name=label, tag=label)
-            dst = products[s // 2][:, s % 2]
+                products[s // SLOTS] = keep.tile([P, SLOTS, HEADS, 2, D], F32, name=label, tag=label)
+            dst = products[s // SLOTS][:, j]
             if s < PLAIN_STEPS:
                 nc.vector.tensor_tensor(
                     out=dst,
-                    in0=sums[s][:].rearrange("p (h d) -> p h d", d=D).unsqueeze(2).to_broadcast([P, HEADS, 2, D]),
-                    in1=trig[:, j].unsqueeze(1).to_broadcast([P, HEADS, 2, D]),
+                    in0=trig[:, j].unsqueeze(1).to_broadcast([P, HEADS, 2, D]),
+                    in1=sums[s][:].rearrange("p (h d) -> p h d", d=D).unsqueeze(2).to_broadcast([P, HEADS, 2, D]),
                     op=ALU.mult,
                 )
             else:
                 for h in range(HEADS):
                     nc.vector.scalar_tensor_tensor(
                         out=dst[:, h],
-                        in0=sums[s][:, h * D : (h + 1) * D].unsqueeze(1).to_broadcast([P, 2, D]),
+                        in0=trig[:, j],
                         scalar=inv_norm[:, s - PLAIN_STEPS, h : h + 1],
-                        in1=trig[:, j],
+                        in1=sums[s][:, h * D : (h + 1) * D].unsqueeze(1).to_broadcast([P, 2, D]),
                         op0=ALU.mult,
                         op1=ALU.mult,
                     )
 
-        def add_pair(engine, s):
-            group, j = divmod(s - 1, SLOTS)
-            if j == 0 or s == STEPS - 1:
-                label = "staged%d" % (len(stages_taken) % STAGE_BUFS)
-                staged[group] = keep.tile([P, HEADS, SLOTS, D], F32, name=label, tag=label)
-                stages_taken.append(staged[group])
-            pair = products[s // 2]
+        def add_and_store(engine, group, slots):
+            label = "staged%d" % (len(staged) % STAGE_BUFS)
+            rotated = keep.tile([P, HEADS, SLOTS, D], F32, name=label, tag=label)
+            staged.append(rotated)
             for half in range(2):
                 here = slice(half * HALF, (half + 1) * HALF)
                 other = slice((1 - half) * HALF, (2 - half) * HALF)
                 engine.tensor_tensor(
-                    out=staged[group][:, :, j : j + 2, here].rearrange("p h j d -> p j h d"),
-                    in0=pair[:, :, :, 0, here],
-                    in1=pair[:, :, :, 1, other],
+                    out=rotated[:, :, slots, here].rearrange("p h j d -> p j h d"),
+                    in0=products[group][:, slots, :, 0, here],
+                    in1=products[group][:, slots, :, 1, other],
                     op=ALU.add,
                 )
-
-        def store(group, slots):
             c, b = divmod(group, B)
             m, half = divmod(c, 2)
             rows = outs[m][b, half * HEADS : (half + 1) * HEADS, first_row[m] : first_row[m] + N, :]
             rows = rows.rearrange("h (p j) d -> p h j d", j=SLOTS)
             nc.sync.dma_start(
                 out=rows[:, :, slots, :].rearrange("p h j d -> p h (j d)"),
-                in_=staged[group][:, :, slots, :].rearrange("p h j d -> p h (j d)"),
+                in_=rotated[:, :, slots, :].rearrange("p h j d -> p h (j d)"),
             )
 
         def memory_rows():
@@ -246,14 +240,14 @@ def tile_attention_pa_kernel(tc, x, freqs, Wq, Wk, Wv, mem_k, mem_v, out_0, out_
         load_wv(0, 1)
         for i in range(3):
             load_x(i)
-        nc.sync.dma_start(out=memk_raw[:], in_=mem_k.rearrange("h (q m) d -> (h q) m d", q=MEM_Q))
-        nc.sync.dma_start(out=memv_raw[:], in_=mem_v.rearrange("h (q m) d -> (h q) m d", q=MEM_Q))
         load_wv(1, 0)
         for i in range(3, 6):
             load_x(i)
         load_wv(1, 1)
         for i in range(6, TILES):
             load_x(i)
+        nc.sync.dma_start(out=memk_raw[:], in_=mem_k.rearrange("h (q m) d -> (h q) m d", q=MEM_Q))
+        nc.sync.dma_start(out=memv_raw[:], in_=mem_v.rearrange("h (q m) d -> (h q) m d", q=MEM_Q))
         for m in (1, 2):
             for g in range(PASSES):
                 load_wqk(m, g)
@@ -280,9 +274,9 @@ def tile_attention_pa_kernel(tc, x, freqs, Wq, Wk, Wv, mem_k, mem_v, out_0, out_
         pieces = [(c, g, k) for c in range(1, CHUNKS) for g in range(PASSES) for k in range(PIECES)]
         per_chunk = PASSES * PIECES
         piece_step = (
-            [max(n - 2, -1) for n in range(per_chunk)]
-            + [6 + n // 2 for n in range(2 * per_chunk)]
-            + [14 + 3 * n // 2 for n in range(2 * per_chunk)]
+            [n // 2 - 1 for n in range(per_chunk + PIECES)]
+            + [6 + n // 2 for n in range(per_chunk + PIECES)]
+            + [14 + 4 * n // 3 for n in range(2 * per_chunk)]
         )
 
         def interleave_pieces(s):
@@ -292,34 +286,39 @@ def tile_attention_pa_kernel(tc, x, freqs, Wq, Wk, Wv, mem_k, mem_v, out_0, out_
 
         interleave_pieces(-1)
         turn_at = {0: (4, 5), 1: (6,), 2: (7,)}
-        quantize_at = {0: 2, 1: 4, 3: 6}
+        quantize_x_at = {0: 2, 1: 4, 3: 6}
+        quantize_w_at = {2: (1, 0), 3: (1, 1)}
+        for c in range(2, CHUNKS):
+            for g in range(PASSES):
+                quantize_w_at[TILES * (c - 1) - 1 + SLOTS * g] = (c, g)
         for s in range(STEPS):
-            c, i = divmod(s, TILES)
             for t in turn_at.get(s, ()):
                 turn_x(t)
-            if s == 3:
+            if s == 5:
                 memory_rows()
             interleave_pieces(s)
             multiply(s)
-            if s in quantize_at:
-                quantize_x(quantize_at[s], 2)
-            if c + 1 < CHUNKS and i in (3, 5):
-                quantize_w(c + 1, (i - 3) // 2)
-            if s % 2 == 1:
-                add_pair(nc.vector if s == STEPS - 1 else nc.gpsimd, s)
-            if s == STEPS - 3:
-                store(s // SLOTS, slice(0, 2))
-            elif s == STEPS - 1:
-                store(s // SLOTS, slice(2, SLOTS))
+            if s in quantize_x_at:
+                quantize_x(quantize_x_at[s], 2)
+            if s in quantize_w_at:
+                quantize_w(*quantize_w_at[s])
+            if s == STEPS - 1:
+                add_and_store(nc.vector, s // SLOTS, slice(0, 2))
+                add_and_store(nc.vector, s // SLOTS, slice(2, SLOTS))
             elif s % SLOTS == SLOTS - 1:
-                store(s // SLOTS, slice(0, SLOTS))
-            if s + 2 < STEPS:
+                add_and_store(nc.gpsimd, s // SLOTS, slice(0, SLOTS))
+            if s + 2 < PLAIN_STEPS:
                 project(s + 2)
-            if PLAIN_STEPS <= s + 2 < STEPS:
-                sum_squares(s + 2, range(0, HEADS // 2))
-            if PLAIN_STEPS <= s + 1 < STEPS:
-                above_floor(excess[:, s + 1 - PLAIN_STEPS, :], sumsq[:, s + 1 - PLAIN_STEPS, :])
-            if PLAIN_STEPS <= s + 2 < STEPS:
-                sum_squares(s + 2, range(HEADS // 2, HEADS))
-            if PLAIN_STEPS <= s + 1 < STEPS:
-                inverse_root(inv_norm[:, s + 1 - PLAIN_STEPS, :], excess[:, s + 1 - PLAIN_STEPS, :])
+            ahead = s + 3
+            normed = PLAIN_STEPS <= ahead < STEPS
+            pair = slice(s + 1 - PLAIN_STEPS, s + 3 - PLAIN_STEPS)
+            roots = s % 2 == 1 and PLAIN_STEPS <= s + 1 < STEPS
+            if normed:
+                project(ahead)
+                sum_squares(ahead, range(0, HEADS // 2))
+            if roots:
+                above_floor(excess[:, pair, :], sumsq[:, pair, :])
+            if normed:
+                sum_squares(ahead, range(HEADS // 2, HEADS))
+            if roots:
+                inverse_root(inv_norm[:, pair, :], excess[:, pair, :])

@@ -33,6 +33,7 @@ EPS_SQ = 1e-24
 MEM_Q = 4
 MEM_ROWS = MEM // MEM_Q
 BANKS = 8
+TAIL_HEADS = 2
 GROUPED_BUFS = 4
 PROD_BUFS = 3
 STAGE_BUFS = 4
@@ -78,7 +79,7 @@ def tile_attention_pa_kernel(tc, x, freqs, Wq, Wk, Wv, mem_k, mem_v, out_0, out_
         grouped = {}
         sums = {}
         products = {}
-        staged = []
+        staged = {}
 
         def take_bank():
             label = "bank%d" % (len(banks_taken) % BANKS)
@@ -195,26 +196,26 @@ def tile_attention_pa_kernel(tc, x, freqs, Wq, Wk, Wv, mem_k, mem_v, out_0, out_
                         op1=ALU.mult,
                     )
 
-        def add_and_store(engine, group, slots):
-            label = "staged%d" % (len(staged) % STAGE_BUFS)
-            rotated = keep.tile([P, HEADS, SLOTS, D], F32, name=label, tag=label)
-            staged.append(rotated)
+        def add_and_store(engine, group, heads):
+            if group not in staged:
+                label = "staged%d" % (group % STAGE_BUFS)
+                staged[group] = keep.tile([P, HEADS, SLOTS, D], F32, name=label, tag=label)
+            rotated = staged[group]
             for half in range(2):
                 here = slice(half * HALF, (half + 1) * HALF)
                 other = slice((1 - half) * HALF, (2 - half) * HALF)
                 engine.tensor_tensor(
-                    out=rotated[:, :, slots, here].rearrange("p h j d -> p j h d"),
-                    in0=products[group][:, slots, :, 0, here],
-                    in1=products[group][:, slots, :, 1, other],
+                    out=rotated[:, heads, :, here].rearrange("p h j d -> p j h d"),
+                    in0=products[group][:, :, heads, 0, here],
+                    in1=products[group][:, :, heads, 1, other],
                     op=ALU.add,
                 )
             c, b = divmod(group, B)
             m, half = divmod(c, 2)
             rows = outs[m][b, half * HEADS : (half + 1) * HEADS, first_row[m] : first_row[m] + N, :]
-            rows = rows.rearrange("h (p j) d -> p h j d", j=SLOTS)
             nc.sync.dma_start(
-                out=rows[:, :, slots, :].rearrange("p h j d -> p h (j d)"),
-                in_=rotated[:, :, slots, :].rearrange("p h j d -> p h (j d)"),
+                out=rows[heads].rearrange("h (p j) d -> p h (j d)", j=SLOTS),
+                in_=rotated[:, heads].rearrange("p h j d -> p h (j d)"),
             )
 
         def memory_rows():
@@ -238,10 +239,10 @@ def tile_attention_pa_kernel(tc, x, freqs, Wq, Wk, Wv, mem_k, mem_v, out_0, out_
         nc.sync.dma_start(out=angles[:], in_=freqs.rearrange("(p j) d -> p j d", j=SLOTS))
         load_wv(0, 0)
         load_wv(0, 1)
-        for i in range(3):
+        for i in range(4):
             load_x(i)
         load_wv(1, 0)
-        for i in range(3, 6):
+        for i in range(4, 6):
             load_x(i)
         load_wv(1, 1)
         for i in range(6, TILES):
@@ -260,21 +261,24 @@ def tile_attention_pa_kernel(tc, x, freqs, Wq, Wk, Wv, mem_k, mem_v, out_0, out_
         nc.scalar.activation(out=trig[:, :, 0, :], in_=abs_angles[:], func=ACT.Sin, scale=-1.0, bias=math.pi / 2)
 
         for g in range(PASSES):
-            interleave_w(nc.vector.tensor_copy, 0, g, 0, COLS)
+            interleave_w(nc.vector.tensor_copy, 0, g, 0, COLS // 2)
+            interleave_w(nc.scalar.copy, 0, g, COLS // 2, COLS // 2)
         for i in range(3):
             turn_x(i)
         for g in range(PASSES):
             quantize_w(0, g)
         quantize_x(0, 1)
-        quantize_x(1, 1)
         project(0)
+        quantize_x(1, 1)
         turn_x(3)
         project(1)
 
-        pieces = [(c, g, k) for c in range(1, CHUNKS) for g in range(PASSES) for k in range(PIECES)]
+        pieces = [(1, g, k) for g in range(PASSES) for k in range(PIECES // 2)]
+        pieces = pieces + [(c, g, k) for c in range(2, CHUNKS) for g in range(PASSES) for k in range(PIECES)]
         per_chunk = PASSES * PIECES
         piece_step = (
-            [n // 2 - 1 for n in range(per_chunk + PIECES)]
+            [-1, 0, 1, 1]
+            + [3 + n // 2 for n in range(PIECES)]
             + [6 + n // 2 for n in range(per_chunk + PIECES)]
             + [14 + 4 * n // 3 for n in range(2 * per_chunk)]
         )
@@ -286,8 +290,8 @@ def tile_attention_pa_kernel(tc, x, freqs, Wq, Wk, Wv, mem_k, mem_v, out_0, out_
 
         interleave_pieces(-1)
         turn_at = {0: (4, 5), 1: (6,), 2: (7,)}
-        quantize_x_at = {0: 2, 1: 4, 3: 6}
-        quantize_w_at = {2: (1, 0), 3: (1, 1)}
+        quantize_x_at = {0: 2, 1: 4, 2: 6}
+        quantize_w_at = {}
         for c in range(2, CHUNKS):
             for g in range(PASSES):
                 quantize_w_at[TILES * (c - 1) - 1 + SLOTS * g] = (c, g)
@@ -298,15 +302,23 @@ def tile_attention_pa_kernel(tc, x, freqs, Wq, Wk, Wv, mem_k, mem_v, out_0, out_
                 memory_rows()
             interleave_pieces(s)
             multiply(s)
+            if s in (1, 2):
+                interleave_w(nc.vector.tensor_copy, 1, s - 1, COLS // 2, COLS // 2)
+            if s == 2:
+                quantize_w(1, 0)
+                quantize_w(1, 1)
             if s in quantize_x_at:
                 quantize_x(quantize_x_at[s], 2)
             if s in quantize_w_at:
                 quantize_w(*quantize_w_at[s])
             if s == STEPS - 1:
-                add_and_store(nc.vector, s // SLOTS, slice(0, 2))
-                add_and_store(nc.vector, s // SLOTS, slice(2, SLOTS))
+                for h in range(0, HEADS, TAIL_HEADS):
+                    add_and_store(nc.vector, s // SLOTS, slice(h, h + TAIL_HEADS))
+            elif s == STEPS - 1 - SLOTS:
+                add_and_store(nc.gpsimd, s // SLOTS, slice(0, HEADS // 2))
+                add_and_store(nc.gpsimd, s // SLOTS, slice(HEADS // 2, HEADS))
             elif s % SLOTS == SLOTS - 1:
-                add_and_store(nc.gpsimd, s // SLOTS, slice(0, SLOTS))
+                add_and_store(nc.gpsimd, s // SLOTS, slice(0, HEADS))
             if s + 2 < PLAIN_STEPS:
                 project(s + 2)
             ahead = s + 3

@@ -176,8 +176,8 @@ def tile_attention_pa_kernel(tc, x, freqs, Wq, Wk, Wv, mem_k, mem_v, out_0, out_
             j = s % SLOTS
             if j == 0:
                 label = "products%d" % (len(products) % PROD_BUFS)
-                products[s // SLOTS] = keep.tile([P, SLOTS, HEADS, 2, D], F32, name=label, tag=label)
-            dst = products[s // SLOTS][:, j]
+                products[s // SLOTS] = keep.tile([P, HEADS, SLOTS, 2, D], F32, name=label, tag=label)
+            dst = products[s // SLOTS][:, :, j]
             if s < PLAIN_STEPS:
                 nc.vector.tensor_tensor(
                     out=dst,
@@ -201,15 +201,13 @@ def tile_attention_pa_kernel(tc, x, freqs, Wq, Wk, Wv, mem_k, mem_v, out_0, out_
                 label = "staged%d" % (group % STAGE_BUFS)
                 staged[group] = keep.tile([P, HEADS, SLOTS, D], F32, name=label, tag=label)
             rotated = staged[group]
-            for half in range(2):
-                here = slice(half * HALF, (half + 1) * HALF)
-                other = slice((1 - half) * HALF, (2 - half) * HALF)
-                engine.tensor_tensor(
-                    out=rotated[:, heads, :, here].rearrange("p h j d -> p j h d"),
-                    in0=products[group][:, :, heads, 0, here],
-                    in1=products[group][:, :, heads, 1, other],
-                    op=ALU.add,
-                )
+            both = products[group][:, heads].rearrange("p h j s (x e) -> p (h j) s x e", e=HALF)
+            engine.tensor_tensor(
+                out=rotated[:, heads].rearrange("p h j (x e) -> p (h j) x e", e=HALF),
+                in0=both[:, :, 0],
+                in1=both[:, :, 1, ::-1, :],
+                op=ALU.add,
+            )
             c, b = divmod(group, B)
             m, half = divmod(c, 2)
             rows = outs[m][b, half * HEADS : (half + 1) * HEADS, first_row[m] : first_row[m] + N, :]

@@ -24,19 +24,25 @@ SLOTS = N // P
 TILES = B * SLOTS
 COLS = 512
 HEADS = COLS // D
-CHUNKS = 6
+CHUNKS = 3 * H * D // COLS
 STEPS = CHUNKS * TILES
 PLAIN_STEPS = 2 * TILES
+EPS_SQ = 1e-24
+
 PIECE = 128
 PIECES = COLS // PIECE
-EPS_SQ = 1e-24
-MEM_Q = 4
-MEM_ROWS = MEM // MEM_Q
-BANKS = 8
+MEM_PARTS = 4
+MEM_ROWS = MEM // MEM_PARTS
 TAIL_HEADS = 2
+
+PLAIN_AHEAD = 2
+NORM_AHEAD = 3
+MEM_STEP = 5
+
+BANKS = 8
 GROUPED_BUFS = 4
-PROD_BUFS = 3
-STAGE_BUFS = 4
+PRODUCT_BUFS = 3
+ROTATED_BUFS = 4
 
 
 def tile_attention_pa_kernel(tc, x, freqs, Wq, Wk, Wv, mem_k, mem_v, out_0, out_1, out_2):
@@ -66,20 +72,20 @@ def tile_attention_pa_kernel(tc, x, freqs, Wq, Wk, Wv, mem_k, mem_v, out_0, out_
         sumsq = keep.tile([P, STEPS - PLAIN_STEPS, HEADS], F32)
         excess = keep.tile([P, STEPS - PLAIN_STEPS, HEADS], F32)
         inv_norm = keep.tile([P, STEPS - PLAIN_STEPS, HEADS], F32)
-        memk_raw = keep.tile([H * MEM_Q, MEM_ROWS, D], BF16)
-        memv_raw = keep.tile([H * MEM_Q, MEM_ROWS, D], BF16)
-        memk_sq = keep.tile([H * MEM_Q, MEM_ROWS, D], F32)
-        memk_out = keep.tile([H * MEM_Q, MEM_ROWS, D], F32)
-        memv_out = keep.tile([H * MEM_Q, MEM_ROWS, D], F32)
-        memk_sumsq = keep.tile([H * MEM_Q, MEM_ROWS], F32)
-        memk_excess = keep.tile([H * MEM_Q, MEM_ROWS], F32)
-        memk_inv = keep.tile([H * MEM_Q, MEM_ROWS], F32)
+        memk_raw = keep.tile([H * MEM_PARTS, MEM_ROWS, D], BF16)
+        memv_raw = keep.tile([H * MEM_PARTS, MEM_ROWS, D], BF16)
+        memk_squares = keep.tile([H * MEM_PARTS, MEM_ROWS, D], F32)
+        memk_out = keep.tile([H * MEM_PARTS, MEM_ROWS, D], F32)
+        memv_out = keep.tile([H * MEM_PARTS, MEM_ROWS, D], F32)
+        memk_sumsq = keep.tile([H * MEM_PARTS, MEM_ROWS], F32)
+        memk_excess = keep.tile([H * MEM_PARTS, MEM_ROWS], F32)
+        memk_inv = keep.tile([H * MEM_PARTS, MEM_ROWS], F32)
 
         banks_taken = []
         grouped = {}
         sums = {}
         products = {}
-        staged = {}
+        rotated = {}
 
         def take_bank():
             label = "bank%d" % (len(banks_taken) % BANKS)
@@ -173,11 +179,11 @@ def tile_attention_pa_kernel(tc, x, freqs, Wq, Wk, Wv, mem_k, mem_v, out_0, out_
             nc.scalar.activation(out=dst, in_=src, func=ACT.Abs_reciprocal_sqrt, bias=EPS_SQ)
 
         def multiply(s):
-            j = s % SLOTS
+            group, j = divmod(s, SLOTS)
             if j == 0:
-                label = "products%d" % (len(products) % PROD_BUFS)
-                products[s // SLOTS] = keep.tile([P, HEADS, SLOTS, 2, D], F32, name=label, tag=label)
-            dst = products[s // SLOTS][:, :, j]
+                label = "products%d" % (group % PRODUCT_BUFS)
+                products[group] = keep.tile([P, HEADS, SLOTS, 2, D], F32, name=label, tag=label)
+            dst = products[group][:, :, j]
             if s < PLAIN_STEPS:
                 nc.vector.tensor_tensor(
                     out=dst,
@@ -197,13 +203,12 @@ def tile_attention_pa_kernel(tc, x, freqs, Wq, Wk, Wv, mem_k, mem_v, out_0, out_
                     )
 
         def add_and_store(engine, group, heads):
-            if group not in staged:
-                label = "staged%d" % (group % STAGE_BUFS)
-                staged[group] = keep.tile([P, HEADS, SLOTS, D], F32, name=label, tag=label)
-            rotated = staged[group]
-            both = products[group][:, heads].rearrange("p h j s (x e) -> p (h j) s x e", e=HALF)
+            if group not in rotated:
+                label = "rotated%d" % (group % ROTATED_BUFS)
+                rotated[group] = keep.tile([P, HEADS, SLOTS, D], F32, name=label, tag=label)
+            both = products[group][:, heads].rearrange("p h j s (y e) -> p (h j) s y e", e=HALF)
             engine.tensor_tensor(
-                out=rotated[:, heads].rearrange("p h j (x e) -> p (h j) x e", e=HALF),
+                out=rotated[group][:, heads].rearrange("p h j (y e) -> p (h j) y e", e=HALF),
                 in0=both[:, :, 0],
                 in1=both[:, :, 1, ::-1, :],
                 op=ALU.add,
@@ -213,13 +218,16 @@ def tile_attention_pa_kernel(tc, x, freqs, Wq, Wk, Wv, mem_k, mem_v, out_0, out_
             rows = outs[m][b, half * HEADS : (half + 1) * HEADS, first_row[m] : first_row[m] + N, :]
             nc.sync.dma_start(
                 out=rows[heads].rearrange("h (p j) d -> p h (j d)", j=SLOTS),
-                in_=rotated[:, heads].rearrange("p h j d -> p h (j d)"),
+                in_=rotated[group][:, heads].rearrange("p h j d -> p h (j d)"),
             )
 
         def memory_rows():
             for r in range(MEM_ROWS):
                 nc.scalar.activation(
-                    out=memk_sq[:, r, :], in_=memk_raw[:, r, :], func=ACT.Square, accum_out=memk_sumsq[:, r : r + 1]
+                    out=memk_squares[:, r, :],
+                    in_=memk_raw[:, r, :],
+                    func=ACT.Square,
+                    accum_out=memk_sumsq[:, r : r + 1],
                 )
             nc.scalar.copy(out=memv_out[:], in_=memv_raw[:])
             above_floor(memk_excess[:], memk_sumsq[:])
@@ -229,24 +237,22 @@ def tile_attention_pa_kernel(tc, x, freqs, Wq, Wk, Wv, mem_k, mem_v, out_0, out_
                     out=memk_out[:, r, :], in_=memk_raw[:, r, :], func=ACT.Copy, scale=memk_inv[:, r : r + 1]
                 )
             for dst, src in ((out_2, memv_out), (out_1, memk_out)):
-                for q in range(MEM_Q):
+                for q in range(MEM_PARTS):
                     rows = dst[:, :, q * MEM_ROWS : (q + 1) * MEM_ROWS, :].rearrange("b h m d -> h b (m d)")
-                    part = src[q : H * MEM_Q : MEM_Q].rearrange("h m d -> h (m d)")
+                    part = src[q : H * MEM_PARTS : MEM_PARTS].rearrange("h m d -> h (m d)")
                     nc.sync.dma_start(out=rows, in_=part.unsqueeze(1).to_broadcast([H, B, MEM_ROWS * D]))
 
         nc.sync.dma_start(out=angles[:], in_=freqs.rearrange("(p j) d -> p j d", j=SLOTS))
         load_wv(0, 0)
         load_wv(0, 1)
-        for i in range(4):
+        for i in range(SLOTS):
             load_x(i)
-        load_wv(1, 0)
-        for i in range(4, 6):
-            load_x(i)
-        load_wv(1, 1)
-        for i in range(6, TILES):
-            load_x(i)
-        nc.sync.dma_start(out=memk_raw[:], in_=mem_k.rearrange("h (q m) d -> (h q) m d", q=MEM_Q))
-        nc.sync.dma_start(out=memv_raw[:], in_=mem_v.rearrange("h (q m) d -> (h q) m d", q=MEM_Q))
+        for g in range(PASSES):
+            load_wv(1, g)
+            load_x(SLOTS + 2 * g)
+            load_x(SLOTS + 2 * g + 1)
+        nc.sync.dma_start(out=memk_raw[:], in_=mem_k.rearrange("h (q m) d -> (h q) m d", q=MEM_PARTS))
+        nc.sync.dma_start(out=memv_raw[:], in_=mem_v.rearrange("h (q m) d -> (h q) m d", q=MEM_PARTS))
         for m in (1, 2):
             for g in range(PASSES):
                 load_wqk(m, g)
@@ -270,65 +276,64 @@ def tile_attention_pa_kernel(tc, x, freqs, Wq, Wk, Wv, mem_k, mem_v, out_0, out_
         quantize_x(1, 1)
         turn_x(3)
         project(1)
+        interleave_w(nc.scalar.copy, 1, 0, 0, PIECE)
 
-        pieces = [(1, g, k) for g in range(PASSES) for k in range(PIECES // 2)]
-        pieces = pieces + [(c, g, k) for c in range(2, CHUNKS) for g in range(PASSES) for k in range(PIECES)]
-        per_chunk = PASSES * PIECES
-        piece_step = (
-            [-1, 0, 1, 1]
-            + [3 + n // 2 for n in range(PIECES)]
-            + [6 + n // 2 for n in range(per_chunk + PIECES)]
-            + [14 + 4 * n // 3 for n in range(2 * per_chunk)]
-        )
+        first_norm_step = PLAIN_STEPS - NORM_AHEAD
+        pieces = [(c, g, k) for c in range(2, CHUNKS) for g in range(PASSES) for k in range(PIECES)]
+        piece_steps = sorted(2 * [s for s in range(SLOTS - 1, first_norm_step + 1) if s != MEM_STEP])
+        piece_steps = piece_steps + [first_norm_step + 2 * n for n in range(len(pieces) - len(piece_steps))]
+        pieces_at = {0: [(1, 0, 1)], 1: [(1, 1, 0), (1, 1, 1)]}
+        for s, piece in zip(piece_steps, pieces):
+            pieces_at.setdefault(s, []).append(piece)
 
-        def interleave_pieces(s):
-            for n, (c, g, k) in enumerate(pieces):
-                if piece_step[n] == s:
-                    interleave_w(nc.scalar.copy, c, g, k * PIECE, PIECE)
-
-        interleave_pieces(-1)
         turn_at = {0: (4, 5), 1: (6,), 2: (7,)}
-        quantize_x_at = {0: 2, 1: 4, 2: 6}
         quantize_w_at = {}
         for c in range(2, CHUNKS):
             for g in range(PASSES):
                 quantize_w_at[TILES * (c - 1) - 1 + SLOTS * g] = (c, g)
+
         for s in range(STEPS):
-            for t in turn_at.get(s, ()):
-                turn_x(t)
-            if s == 5:
+            group = s // SLOTS
+            for i in turn_at.get(s, ()):
+                turn_x(i)
+            if s == MEM_STEP:
                 memory_rows()
-            interleave_pieces(s)
+            for c, g, k in pieces_at.get(s, ()):
+                interleave_w(nc.scalar.copy, c, g, k * PIECE, PIECE)
+
             multiply(s)
             if s in (1, 2):
                 interleave_w(nc.vector.tensor_copy, 1, s - 1, COLS // 2, COLS // 2)
             if s == 2:
                 quantize_w(1, 0)
                 quantize_w(1, 1)
-            if s in quantize_x_at:
-                quantize_x(quantize_x_at[s], 2)
+            if s < SLOTS - 1:
+                quantize_x(2 * s + 2, 2)
             if s in quantize_w_at:
                 quantize_w(*quantize_w_at[s])
+
             if s == STEPS - 1:
                 for h in range(0, HEADS, TAIL_HEADS):
-                    add_and_store(nc.vector, s // SLOTS, slice(h, h + TAIL_HEADS))
+                    add_and_store(nc.vector, group, slice(h, h + TAIL_HEADS))
             elif s == STEPS - 1 - SLOTS:
-                add_and_store(nc.gpsimd, s // SLOTS, slice(0, HEADS // 2))
-                add_and_store(nc.gpsimd, s // SLOTS, slice(HEADS // 2, HEADS))
+                add_and_store(nc.gpsimd, group, slice(0, HEADS // 2))
+                add_and_store(nc.gpsimd, group, slice(HEADS // 2, HEADS))
             elif s % SLOTS == SLOTS - 1:
-                add_and_store(nc.gpsimd, s // SLOTS, slice(0, HEADS))
-            if s + 2 < PLAIN_STEPS:
-                project(s + 2)
-            ahead = s + 3
+                add_and_store(nc.gpsimd, group, slice(0, HEADS))
+
+            if s + PLAIN_AHEAD < PLAIN_STEPS:
+                project(s + PLAIN_AHEAD)
+
+            ahead = s + NORM_AHEAD
             normed = PLAIN_STEPS <= ahead < STEPS
+            roots_due = s % 2 == 1 and PLAIN_STEPS <= s + 1 < STEPS
             pair = slice(s + 1 - PLAIN_STEPS, s + 3 - PLAIN_STEPS)
-            roots = s % 2 == 1 and PLAIN_STEPS <= s + 1 < STEPS
             if normed:
                 project(ahead)
                 sum_squares(ahead, range(0, HEADS // 2))
-            if roots:
+            if roots_due:
                 above_floor(excess[:, pair, :], sumsq[:, pair, :])
             if normed:
                 sum_squares(ahead, range(HEADS // 2, HEADS))
-            if roots:
+            if roots_due:
                 inverse_root(inv_norm[:, pair, :], excess[:, pair, :])

import math
from contextlib import ExitStack

import concourse.mybir as mybir
from concourse.masks import make_identity

B, N, DIM, H, D, MEM = 2, 512, 1024, 16, 64, 16
FLOPS = 2 * B * N * DIM * 3 * H * D

F32 = mybir.dt.float32
BF16 = mybir.dt.bfloat16
U32 = mybir.dt.uint32
U8 = mybir.dt.uint8
E5M2X4 = mybir.dt.float8_e5m2_x4
ACT = mybir.ActivationFunctionType
ALU = mybir.AluOpType

P = 128
PACK = 4
K_PASS = P * PACK
PASSES = DIM // K_PASS
HALF = D // 2
SLOTS = N // P
TILES = B * SLOTS
COLS = 512
HEADS = COLS // D
CHUNKS = 3 * H * D // COLS
STEPS = CHUNKS * TILES
PLAIN_STEPS = 2 * TILES
EPS_SQ = 1e-24

PIECE = 128
PIECES = COLS // PIECE
MEM_PARTS = 4
MEM_ROWS = MEM // MEM_PARTS
TAIL_HEADS = 2

PLAIN_AHEAD = 2
NORM_AHEAD = 3
MEM_STEP = 5

BANKS = 8
GROUPED_BUFS = 4
PRODUCT_BUFS = 3
ROTATED_BUFS = 4


def tile_attention_pa_kernel(tc, x, freqs, Wq, Wk, Wv, mem_k, mem_v, out_0, out_1, out_2):
    nc = tc.nc
    weights = [Wv, Wq, Wk]
    outs = [out_2, out_0, out_1]
    first_row = [MEM, 0, MEM]

    with ExitStack() as ctx:
        keep = ctx.enter_context(tc.tile_pool(name="keep", bufs=1))
        psum = ctx.enter_context(tc.psum_pool(name="psum", bufs=1))
        ctx.enter_context(tc.manual_schedule())

        angles = keep.tile([P, SLOTS, D], BF16)
        abs_angles = keep.tile([P, SLOTS, D], F32)
        trig = keep.tile([P, SLOTS, 2, D], F32)
        ident = keep.tile([P, P], F32)
        x_raw = keep.tile([P, TILES, DIM], BF16)
        x_grouped = keep.tile([P, TILES, DIM], BF16, align_bytes=64)
        x_codes = keep.tile([P, TILES, PASSES * P], U32, align_bytes=64)
        x_scales = keep.tile([P, TILES, PASSES * P], U8, align_bytes=64)
        wv_raw = keep.tile([P, 2, PASSES, PACK, COLS], BF16)
        wqk_raw = keep.tile([P, 2, PASSES, PACK, DIM], BF16)
        w_codes = keep.tile([P, CHUNKS, PASSES, COLS], U32, align_bytes=64)
        w_scales = keep.tile([P, CHUNKS, PASSES, COLS], U8, align_bytes=64)
        squares = keep.tile([P, 2, COLS], F32)
        sumsq = keep.tile([P, STEPS - PLAIN_STEPS, HEADS], F32)
        excess = keep.tile([P, STEPS - PLAIN_STEPS, HEADS], F32)
        inv_norm = keep.tile([P, STEPS - PLAIN_STEPS, HEADS], F32)
        memk_raw = keep.tile([H * MEM_PARTS, MEM_ROWS, D], BF16)
        memv_raw = keep.tile([H * MEM_PARTS, MEM_ROWS, D], BF16)
        memk_squares = keep.tile([H * MEM_PARTS, MEM_ROWS, D], F32)
        memk_out = keep.tile([H * MEM_PARTS, MEM_ROWS, D], F32)
        memv_out = keep.tile([H * MEM_PARTS, MEM_ROWS, D], F32)
        memk_sumsq = keep.tile([H * MEM_PARTS, MEM_ROWS], F32)
        memk_excess = keep.tile([H * MEM_PARTS, MEM_ROWS], F32)
        memk_inv = keep.tile([H * MEM_PARTS, MEM_ROWS], F32)

        banks_taken = []
        grouped = {}
        sums = {}
        products = {}
        rotated = {}

        def take_bank():
            label = "bank%d" % (len(banks_taken) % BANKS)
            bank = psum.tile([P, COLS], F32, name=label, tag=label)
            banks_taken.append(bank)
            return bank

        def load_x(i):
            b, j = divmod(i, SLOTS)
            rows = x[b].rearrange("(p j) k -> p j k", j=SLOTS)
            nc.sync.dma_start(out=x_raw[:, i, :], in_=rows[:, j, :])

        def w_rows(m, g):
            return weights[m][g * K_PASS : (g + 1) * K_PASS, :].rearrange("(p t) n -> p t n", t=PACK)

        def load_wv(half, g):
            nc.sync.dma_start(out=wv_raw[:, half, g], in_=w_rows(0, g)[:, :, half * COLS : (half + 1) * COLS])

        def load_wqk(m, g):
            nc.sync.dma_start(out=wqk_raw[:, m - 1, g], in_=w_rows(m, g))

        def turn_x(i):
            bank = take_bank()
            words = x_raw[:, i, :].bitcast(F32)
            for g in range(PASSES):
                for u in range(2):
                    at = (2 * g + u) * P
                    nc.tensor.transpose(
                        bank[:, at : at + P], words[:, 2 * P * g + u : 2 * P * (g + 1) : 2], ident[:]
                    )
            nc.scalar.copy(
                out=x_grouped[:, i, :].bitcast(F32).rearrange("p (g r u) -> p g r u", g=PASSES, u=2),
                in_=bank[:].rearrange("p (g u r) -> p g r u", g=PASSES, u=2),
            )

        def quantize_x(i, count):
            nc.vector.quantize_mx(
                out=x_codes[:, i : i + count, :].rearrange("p i w -> p (i w)").bitcast(E5M2X4),
                scales=x_scales[:, i : i + count, :].rearrange("p i w -> p (i w)"),
                in_=x_grouped[:, i : i + count, :].rearrange("p i k -> p (i k)"),
            )

        def interleave_w(copy, c, g, start, width):
            if (c, g) not in grouped:
                label = "grouped%d" % (len(grouped) % GROUPED_BUFS)
                grouped[(c, g)] = keep.tile([P, COLS, PACK], BF16, name=label, tag=label, align_bytes=64)
            m, half = divmod(c, 2)
            if m == 0:
                src = wv_raw[:, half, g, :, start : start + width]
            else:
                src = wqk_raw[:, m - 1, g, :, half * COLS + start : half * COLS + start + width]
            copy(
                out=grouped[(c, g)][:, start : start + width, :].rearrange("p (c i) t -> p c t i", i=4),
                in_=src.rearrange("p t (c i) -> p c t i", i=4),
            )

        def quantize_w(c, g):
            nc.vector.quantize_mx(
                out=w_codes[:, c, g, :].bitcast(E5M2X4),
                scales=w_scales[:, c, g, :],
                in_=grouped[(c, g)][:].rearrange("p n t -> p (n t)"),
            )

        def project(s):
            c, i = divmod(s, TILES)
            sums[s] = take_bank()
            for g in range(PASSES):
                nc.tensor.matmul_mx(
                    out=sums[s][:],
                    lhsT=x_codes[:, i, g * P : (g + 1) * P].bitcast(E5M2X4),
                    lhsT_scale=x_scales[:, i, g * P : (g + 1) * P],
                    rhs=w_codes[:, c, g, :].bitcast(E5M2X4),
                    rhs_scale=w_scales[:, c, g, :],
                    start=(g == 0),
                    stop=(g == PASSES - 1),
                )

        def sum_squares(s, heads):
            for h in heads:
                nc.scalar.activation(
                    out=squares[:, s % 2, h * D : (h + 1) * D],
                    in_=sums[s][:, h * D : (h + 1) * D],
                    func=ACT.Square,
                    accum_out=sumsq[:, s - PLAIN_STEPS, h : h + 1],
                )

        def above_floor(dst, src):
            nc.scalar.activation(out=dst, in_=src, func=ACT.Relu, bias=-EPS_SQ)

        def inverse_root(dst, src):
            nc.scalar.activation(out=dst, in_=src, func=ACT.Abs_reciprocal_sqrt, bias=EPS_SQ)

        def multiply(s):
            group, j = divmod(s, SLOTS)
            if j == 0:
                label = "products%d" % (group % PRODUCT_BUFS)
                products[group] = keep.tile([P, HEADS, SLOTS, 2, D], F32, name=label, tag=label)
            dst = products[group][:, :, j]
            if s < PLAIN_STEPS:
                nc.vector.tensor_tensor(
                    out=dst,
                    in0=trig[:, j].unsqueeze(1).to_broadcast([P, HEADS, 2, D]),
                    in1=sums[s][:].rearrange("p (h d) -> p h d", d=D).unsqueeze(2).to_broadcast([P, HEADS, 2, D]),
                    op=ALU.mult,
                )
            else:
                for h in range(HEADS):
                    nc.vector.scalar_tensor_tensor(
                        out=dst[:, h],
                        in0=trig[:, j],
                        scalar=inv_norm[:, s - PLAIN_STEPS, h : h + 1],
                        in1=sums[s][:, h * D : (h + 1) * D].unsqueeze(1).to_broadcast([P, 2, D]),
                        op0=ALU.mult,
                        op1=ALU.mult,
                    )

        def add_and_store(engine, group, heads):
            if group not in rotated:
                label = "rotated%d" % (group % ROTATED_BUFS)
                rotated[group] = keep.tile([P, HEADS, SLOTS, D], F32, name=label, tag=label)
            both = products[group][:, heads].rearrange("p h j s (y e) -> p (h j) s y e", e=HALF)
            engine.tensor_tensor(
                out=rotated[group][:, heads].rearrange("p h j (y e) -> p (h j) y e", e=HALF),
                in0=both[:, :, 0],
                in1=both[:, :, 1, ::-1, :],
                op=ALU.add,
            )
            c, b = divmod(group, B)
            m, half = divmod(c, 2)
            rows = outs[m][b, half * HEADS : (half + 1) * HEADS, first_row[m] : first_row[m] + N, :]
            nc.sync.dma_start(
                out=rows[heads].rearrange("h (p j) d -> p h (j d)", j=SLOTS),
                in_=rotated[group][:, heads].rearrange("p h j d -> p h (j d)"),
            )

        def memory_rows():
            for r in range(MEM_ROWS):
                nc.scalar.activation(
                    out=memk_squares[:, r, :],
                    in_=memk_raw[:, r, :],
                    func=ACT.Square,
                    accum_out=memk_sumsq[:, r : r + 1],
                )
            nc.scalar.copy(out=memv_out[:], in_=memv_raw[:])
            above_floor(memk_excess[:], memk_sumsq[:])
            inverse_root(memk_inv[:], memk_excess[:])
            for r in range(MEM_ROWS):
                nc.scalar.activation(
                    out=memk_out[:, r, :], in_=memk_raw[:, r, :], func=ACT.Copy, scale=memk_inv[:, r : r + 1]
                )
            for dst, src in ((out_2, memv_out), (out_1, memk_out)):
                for q in range(MEM_PARTS):
                    rows = dst[:, :, q * MEM_ROWS : (q + 1) * MEM_ROWS, :].rearrange("b h m d -> h b (m d)")
                    part = src[q : H * MEM_PARTS : MEM_PARTS].rearrange("h m d -> h (m d)")
                    nc.sync.dma_start(out=rows, in_=part.unsqueeze(1).to_broadcast([H, B, MEM_ROWS * D]))

        nc.sync.dma_start(out=angles[:], in_=freqs.rearrange("(p j) d -> p j d", j=SLOTS))
        load_wv(0, 0)
        load_wv(0, 1)
        for i in range(SLOTS):
            load_x(i)
        for g in range(PASSES):
            load_wv(1, g)
            load_x(SLOTS + 2 * g)
            load_x(SLOTS + 2 * g + 1)
        nc.sync.dma_start(out=memk_raw[:], in_=mem_k.rearrange("h (q m) d -> (h q) m d", q=MEM_PARTS))
        nc.sync.dma_start(out=memv_raw[:], in_=mem_v.rearrange("h (q m) d -> (h q) m d", q=MEM_PARTS))
        for m in (1, 2):
            for g in range(PASSES):
                load_wqk(m, g)

        make_identity(nc, ident[:])

        nc.scalar.activation(out=trig[:, :, 1, 0:HALF], in_=angles[:, :, HALF:D], func=ACT.Sin)
        nc.scalar.activation(out=trig[:, :, 1, HALF:D], in_=angles[:, :, 0:HALF], func=ACT.Sin, scale=-1.0)
        nc.scalar.activation(out=abs_angles[:], in_=angles[:], func=ACT.Abs)
        nc.scalar.activation(out=trig[:, :, 0, :], in_=abs_angles[:], func=ACT.Sin, scale=-1.0, bias=math.pi / 2)

        for g in range(PASSES):
            interleave_w(nc.vector.tensor_copy, 0, g, 0, COLS // 2)
            interleave_w(nc.scalar.copy, 0, g, COLS // 2, COLS // 2)
        for i in range(3):
            turn_x(i)
        for g in range(PASSES):
            quantize_w(0, g)
        quantize_x(0, 1)
        project(0)
        quantize_x(1, 1)
        turn_x(3)
        project(1)
        interleave_w(nc.scalar.copy, 1, 0, 0, PIECE)

        first_norm_step = PLAIN_STEPS - NORM_AHEAD
        pieces = [(c, g, k) for c in range(2, CHUNKS) for g in range(PASSES) for k in range(PIECES)]
        piece_steps = sorted(2 * [s for s in range(SLOTS - 1, first_norm_step + 1) if s != MEM_STEP])
        piece_steps = piece_steps + [first_norm_step + 2 * n for n in range(len(pieces) - len(piece_steps))]
        pieces_at = {0: [(1, 0, 1)], 1: [(1, 1, 0), (1, 1, 1)]}
        for s, piece in zip(piece_steps, pieces):
            pieces_at.setdefault(s, []).append(piece)

        turn_at = {0: (4, 5), 1: (6,), 2: (7,)}
        quantize_w_at = {}
        for c in range(2, CHUNKS):
            for g in range(PASSES):
                quantize_w_at[TILES * (c - 1) - 1 + SLOTS * g] = (c, g)

        for s in range(STEPS):
            group = s // SLOTS
            for i in turn_at.get(s, ()):
                turn_x(i)
            if s == MEM_STEP:
                memory_rows()
            for c, g, k in pieces_at.get(s, ()):
                interleave_w(nc.scalar.copy, c, g, k * PIECE, PIECE)

            multiply(s)
            if s in (1, 2):
                interleave_w(nc.vector.tensor_copy, 1, s - 1, COLS // 2, COLS // 2)
            if s == 2:
                quantize_w(1, 0)
                quantize_w(1, 1)
            if s < SLOTS - 1:
                quantize_x(2 * s + 2, 2)
            if s in quantize_w_at:
                quantize_w(*quantize_w_at[s])

            if s == STEPS - 1:
                for h in range(0, HEADS, TAIL_HEADS):
                    add_and_store(nc.vector, group, slice(h, h + TAIL_HEADS))
            elif s == STEPS - 1 - SLOTS:
                add_and_store(nc.gpsimd, group, slice(0, HEADS // 2))
                add_and_store(nc.gpsimd, group, slice(HEADS // 2, HEADS))
            elif s % SLOTS == SLOTS - 1:
                add_and_store(nc.gpsimd, group, slice(0, HEADS))

            if s + PLAIN_AHEAD < PLAIN_STEPS:
                project(s + PLAIN_AHEAD)

            ahead = s + NORM_AHEAD
            normed = PLAIN_STEPS <= ahead < STEPS
            roots_due = s % 2 == 1 and PLAIN_STEPS <= s + 1 < STEPS
            pair = slice(s + 1 - PLAIN_STEPS, s + 3 - PLAIN_STEPS)
            if normed:
                project(ahead)
                sum_squares(ahead, range(0, HEADS // 2))
            if roots_due:
                above_floor(excess[:, pair, :], sumsq[:, pair, :])
            if normed:
                sum_squares(ahead, range(HEADS // 2, HEADS))
            if roots_due:
                inverse_root(inv_norm[:, pair, :], excess[:, pair, :])
